import numpy as np
import ml_dtypes


def mxq(x, axis, fmt="e4m3"):
    dtype, down = {"e4m3": (ml_dtypes.float8_e4m3fn, 7), "e5m2": (ml_dtypes.float8_e5m2, 14)}[fmt]
    v = np.moveaxis(np.asarray(x, np.float32).astype(ml_dtypes.bfloat16).astype(np.float64), axis, -1)
    blocks = v.reshape(v.shape[:-1] + (-1, 32))
    amax = np.abs(blocks).max(-1, keepdims=True)
    byte = np.maximum(np.where(amax > 0, np.frexp(amax)[1] - 1 + 127, 0) - down, 1)
    scale = np.exp2(byte - 127.0)
    codes = (blocks / scale).astype(np.float32).astype(dtype).astype(np.float64)
    return np.moveaxis((codes * scale).reshape(v.shape), -1, axis)


WIDE = False


def mx_kscale(k):
    if not WIDE:
        return np.ones(k)
    levels = np.array([10, -10, 5, -5, 0])
    a = np.random.permutation(np.resize(levels, k // 512 * 4)).reshape(k // 512, 4)
    idx = np.arange(k)
    return np.exp2(a[idx // 512, idx % 128 // 32])


BF16 = ml_dtypes.bfloat16


def bf(x):
    return np.asarray(x, np.float32).astype(BF16)


def f64(x):
    return np.asarray(x).astype(np.float64)


N, D_IN, D_HID, D_OUT = 512, 512, 512, 512


def hamilton_Wq(Wr, Wi, Wj, Wk, xr, xi, xj, xk):
    x_cat = np.concatenate([xr, xi, xj, xk], axis=-1)
    n_in = Wr.shape[1]
    Wq = mxq(np.concatenate([Wr, Wi, Wj, Wk], axis=1), 1, "e4m3")
    Wr, Wi, Wj, Wk = Wq[:, :n_in], Wq[:, n_in:2 * n_in], Wq[:, 2 * n_in:3 * n_in], Wq[:, 3 * n_in:]
    W_block = np.concatenate([
        np.concatenate([Wr, Wi, Wj, Wk], axis=0),
        np.concatenate([-Wi, Wr, -Wk, Wj], axis=0),
        np.concatenate([-Wj, Wk, Wr, -Wi], axis=0),
        np.concatenate([-Wk, -Wj, Wi, Wr], axis=0),
    ], axis=1)
    h = mxq(x_cat, 1, "e4m3") @ W_block.T
    out = Wr.shape[0]
    return h[:, :out], h[:, out:2 * out], h[:, 2 * out:3 * out], h[:, 3 * out:]


def setup_inputs():
    s = mx_kscale(4 * D_IN)[:D_IN]
    t = mx_kscale(4 * D_HID)[:D_HID]
    inp = {}
    for c in "rijk":
        inp["q_" + c] = bf(np.random.standard_normal((N, D_IN)) * s)
    for c in "rijk":
        inp["W1_" + c] = bf(np.random.standard_normal((D_HID, D_IN)) * 0.5 / np.sqrt(D_IN) / s[None, :] * t[:, None])
    for c in "rijk":
        inp["b1_" + c] = bf(((0.0 if c == "r" else 0.2) + 0.1 * np.random.standard_normal(D_HID)) * t)
    for c in "rijk":
        inp["W2_" + c] = bf(np.random.standard_normal((D_OUT, D_HID)) * 0.7 / np.sqrt(D_HID) / t[None, :])
    for c in "rijk":
        inp["b2_" + c] = bf((0.0 if c == "r" else 0.2) + 0.1 * np.random.standard_normal(D_OUT))
    return inp


def reference(q_r, q_i, q_j, q_k,
              W1_r, W1_i, W1_j, W1_k, b1_r, b1_i, b1_j, b1_k,
              W2_r, W2_i, W2_j, W2_k, b2_r, b2_i, b2_j, b2_k):
    hr, hi, hj, hk = hamilton_Wq(f64(W1_r), f64(W1_i), f64(W1_j), f64(W1_k), f64(q_r), f64(q_i), f64(q_j), f64(q_k))
    hr = np.maximum(hr + f64(b1_r), 0.0)
    hi = np.maximum(hi + f64(b1_i), 0.0)
    hj = np.maximum(hj + f64(b1_j), 0.0)
    hk = np.maximum(hk + f64(b1_k), 0.0)
    or_, oi, oj, ok = hamilton_Wq(f64(W2_r), f64(W2_i), f64(W2_j), f64(W2_k), hr, hi, hj, hk)
    return (or_ + f64(b2_r), oi + f64(b2_i), oj + f64(b2_j), ok + f64(b2_k))

@@ -1,0 +1,227 @@
+from contextlib import ExitStack
+
+import concourse.mybir as mybir
+from concourse.masks import make_identity
+
+F32 = mybir.dt.float32
+BF16 = mybir.dt.bfloat16
+U32 = mybir.dt.uint32
+U8 = mybir.dt.uint8
+FP8X4 = mybir.dt.float8_e4m3fn_x4
+
+P = 128
+SIZE = 512
+TILES = SIZE // P
+PACK = 4
+PARTS = 4
+
+FLOPS = 2 * 2 * SIZE * (PARTS * SIZE) * (PARTS * SIZE)
+
+HAMILTON = (
+    ((0, 1), (1, -1), (2, -1), (3, -1)),
+    ((1, 1), (0, 1), (3, 1), (2, -1)),
+    ((2, 1), (3, -1), (0, 1), (1, 1)),
+    ((3, 1), (2, 1), (1, -1), (0, 1)),
+)
+
+
+def tile_qmlp_kernel(
+    tc,
+    q_r, q_i, q_j, q_k,
+    W1_r, W1_i, W1_j, W1_k,
+    b1_r, b1_i, b1_j, b1_k,
+    W2_r, W2_i, W2_j, W2_k,
+    b2_r, b2_i, b2_j, b2_k,
+    out_0, out_1, out_2, out_3,
+):
+    nc = tc.nc
+    q = (q_r, q_i, q_j, q_k)
+    w1 = (W1_r, W1_i, W1_j, W1_k)
+    b1 = (b1_r, b1_i, b1_j, b1_k)
+    w2 = (W2_r, W2_i, W2_j, W2_k)
+    b2 = (b2_r, b2_i, b2_j, b2_k)
+    outs = (out_0, out_1, out_2, out_3)
+
+    with ExitStack() as ctx:
+        const = ctx.enter_context(tc.tile_pool(name="const", bufs=1))
+        raw_pool = ctx.enter_context(tc.tile_pool(name="raw", bufs=1))
+        grouped_pool = ctx.enter_context(tc.tile_pool(name="grouped", bufs=8))
+        planar_pool = ctx.enter_context(tc.tile_pool(name="planar", bufs=2))
+        mx_pool = ctx.enter_context(tc.tile_pool(name="mx", bufs=1))
+        result_pool = ctx.enter_context(tc.tile_pool(name="result", bufs=4))
+        psum = ctx.enter_context(tc.psum_pool(name="psum", bufs=8))
+
+        def load(name, view):
+            raw = raw_pool.tile([P, TILES * SIZE], BF16, name=name)
+            nc.sync.dma_start(out=raw[:].rearrange("p (n x) -> p n x", n=view.shape[1]), in_=view)
+            return raw
+
+        q_raw = []
+        w1_raw = []
+        for c in range(PARTS):
+            q_raw.append(load("q_raw%d" % c, q[c].rearrange("(p a) k -> p a k", a=TILES)))
+            w1_raw.append(
+                load("w1_raw%d" % c, w1[c].rearrange("(u p e) k -> p u (e k)", u=2, e=2))
+            )
+        b1_sb = const.tile([P, PARTS, 16], BF16, name="b1_sb")
+        for c in range(PARTS):
+            nc.sync.dma_start(
+                out=b1_sb[:, c, 0:TILES].rearrange("p (u e) -> p u e", u=2),
+                in_=b1[c].rearrange("(u p e) -> p u e", u=2, e=2),
+            )
+        w2_raw = [
+            load("w2_raw%d" % c, w2[c].rearrange("(a p) k -> p a k", p=P)) for c in range(PARTS)
+        ]
+        b2_sb = const.tile([P, PARTS, SIZE], BF16, name="b2_sb")
+        for c in range(PARTS):
+            nc.sync.dma_start(out=b2_sb[:, c, :], in_=b2[c].partition_broadcast(P))
+
+        ident = const.tile([P, P], F32, name="ident")
+        make_identity(nc, ident[:])
+
+        def transpose_component(raw, name):
+            words = raw[:].bitcast(F32)
+            grouped = grouped_pool.tile(
+                [P, SIZE * PACK], BF16, name=name, tag="grouped", align_bytes=64
+            )
+            grouped_words = grouped[:].bitcast(F32)
+            half = SIZE
+            for b in range(2):
+                bank = psum.tile([P, SIZE], F32, name="%s_bank%d" % (name, b), tag="bank")
+                for u in range(2):
+                    for a2 in range(2):
+                        start = (2 * b + a2) * 2 * P + u * P
+                        nc.tensor.transpose(
+                            bank[:, (2 * u + a2) * P : (2 * u + a2 + 1) * P],
+                            words[:, start : start + P],
+                            ident[:],
+                        )
+                nc.scalar.copy(
+                    out=grouped_words[:, b * half : (b + 1) * half].rearrange(
+                        "p (n u) -> p n u", u=2
+                    ),
+                    in_=bank[:].rearrange("p (u n) -> p n u", u=2),
+                )
+            return grouped
+
+        def negate(grouped, name):
+            minus = grouped_pool.tile(
+                [P, SIZE * PACK], BF16, name=name, tag="grouped", align_bytes=64
+            )
+            nc.vector.tensor_scalar_mul(out=minus[:], in0=grouped[:], scalar1=-1.0)
+            return minus
+
+        def quantise(grouped, name):
+            codes = mx_pool.tile([P, SIZE], U32, name=name + "_codes", align_bytes=64)
+            scales = mx_pool.tile([P, SIZE], U8, name=name + "_scales", align_bytes=64)
+            nc.vector.quantize_mx(out=codes[:].bitcast(FP8X4), scales=scales[:], in_=grouped[:])
+            return codes, scales
+
+        def mx_pass(acc, stationary, tile_index, moving, c):
+            s_codes, s_scales = stationary
+            m_codes, m_scales = moving
+            cols = slice(tile_index * P, (tile_index + 1) * P)
+            nc.tensor.matmul_mx(
+                out=acc[:],
+                lhsT=s_codes[:, cols].bitcast(FP8X4),
+                lhsT_scale=s_scales[:, cols],
+                rhs=m_codes[:].bitcast(FP8X4),
+                rhs_scale=m_scales[:],
+                start=(c == 0),
+                stop=(c == PARTS - 1),
+            )
+
+        q_mx = {}
+        w1_mx = {}
+        w2_mx = {}
+        h_mx = {}
+
+        def layer1_pass(acc, o, t, c):
+            mx_pass(acc, w1_mx[HAMILTON[o][c]], t, q_mx[c], c)
+
+        def layer2_pass(acc, a, o, c):
+            mx_pass(acc, h_mx[c], a, w2_mx[HAMILTON[o][c]], c)
+
+        def hidden_out_of_psum(acc, planar, o, t):
+            nc.scalar.activation(
+                out=planar[:, t, :],
+                in_=acc[:],
+                func=mybir.ActivationFunctionType.Relu,
+                bias=b1_sb[:, o, t : t + 1],
+                scale=1.0,
+            )
+
+        def quantise_hidden(planar, o):
+            grouped = grouped_pool.tile(
+                [P, SIZE * PACK], BF16, name="h_grouped%d" % o, tag="grouped", align_bytes=64
+            )
+            nc.vector.tensor_copy(
+                out=grouped[:].rearrange("p (n i t) -> p n t i", i=4, t=PACK),
+                in_=planar[:].rearrange("p t (n i) -> p n t i", i=4),
+            )
+            h_mx[o] = quantise(grouped, "h%d" % o)
+
+        def prepare_w2(w):
+            grouped = transpose_component(w2_raw[w], "w2_grouped%d" % w)
+            if w > 0:
+                w2_mx[(w, -1)] = quantise(negate(grouped, "w2_minus%d" % w), "w2_minus%d" % w)
+            w2_mx[(w, 1)] = quantise(grouped, "w2_plus%d" % w)
+
+        def store_output(acc, a, o):
+            result = result_pool.tile([P, SIZE], F32, name="result", tag="result")
+            nc.vector.tensor_tensor(
+                out=result[:], in0=acc[:], in1=b2_sb[:, o, :], op=mybir.AluOpType.add
+            )
+            nc.sync.dma_start(
+                out=outs[o].rearrange("(p a) n -> p a n", a=TILES)[:, a, :], in_=result[:]
+            )
+
+        q_grouped = {0: transpose_component(q_raw[0], "q_grouped0")}
+        w1_grouped = {0: transpose_component(w1_raw[0], "w1_grouped0")}
+        acc_r = [psum.tile([P, SIZE], F32, name="acc_r%d" % t, tag="bank") for t in range(TILES)]
+        for c in range(PARTS):
+            if c + 1 < PARTS:
+                q_grouped[c + 1] = transpose_component(q_raw[c + 1], "q_grouped%d" % (c + 1))
+                w1_grouped[c + 1] = transpose_component(w1_raw[c + 1], "w1_grouped%d" % (c + 1))
+            if c > 0:
+                minus = negate(w1_grouped[c], "w1_minus%d" % c)
+            q_mx[c] = quantise(q_grouped[c], "q%d" % c)
+            if c > 0:
+                w1_mx[(c, -1)] = quantise(minus, "w1_minus%d" % c)
+            w1_mx[(c, 1)] = quantise(w1_grouped[c], "w1_plus%d" % c)
+            for t in range(TILES):
+                layer1_pass(acc_r[t], 0, t, c)
+        planar = planar_pool.tile([P, TILES, SIZE], BF16, name="planar", tag="planar")
+        for t in range(TILES):
+            hidden_out_of_psum(acc_r[t], planar, 0, t)
+        quantise_hidden(planar, 0)
+
+        def layer1_component(o):
+            planar = planar_pool.tile([P, TILES, SIZE], BF16, name="planar", tag="planar")
+            for t in range(TILES):
+                acc = psum.tile([P, SIZE], F32, name="acc1", tag="bank")
+                for c in range(PARTS):
+                    layer1_pass(acc, o, t, c)
+                hidden_out_of_psum(acc, planar, o, t)
+            quantise_hidden(planar, o)
+
+        prepare_w2(0)
+        prepare_w2(1)
+        layer1_component(1)
+        prepare_w2(2)
+        prepare_w2(3)
+        layer1_component(2)
+        layer1_component(3)
+
+        acc_0 = [psum.tile([P, SIZE], F32, name="acc_0%d" % o, tag="bank") for o in range(PARTS)]
+        for c in range(PARTS):
+            for o in range(PARTS):
+                layer2_pass(acc_0[o], 0, o, c)
+        for o in range(PARTS):
+            store_output(acc_0[o], 0, o)
+        for a in range(1, TILES):
+            for o in range(PARTS):
+                acc = psum.tile([P, SIZE], F32, name="acc2", tag="bank")
+                for c in range(PARTS):
+                    layer2_pass(acc, a, o, c)
+                store_output(acc, a, o)

@@ -50,6 +50,7 @@ def tile_qmlp_kernel(
         mx_pool = ctx.enter_context(tc.tile_pool(name="mx", bufs=1))
         result_pool = ctx.enter_context(tc.tile_pool(name="result", bufs=4))
         psum = ctx.enter_context(tc.psum_pool(name="psum", bufs=8))
+        ctx.enter_context(tc.manual_schedule())
 
         def load(name, view):
             raw = raw_pool.tile([P, TILES * SIZE], BF16, name=name)

@@ -60,10 +60,10 @@ def tile_qmlp_kernel(
         q_raw = []
         w1_raw = []
         for c in range(PARTS):
-            q_raw.append(load("q_raw%d" % c, q[c].rearrange("(p a) k -> p a k", a=TILES)))
             w1_raw.append(
                 load("w1_raw%d" % c, w1[c].rearrange("(u p e) k -> p u (e k)", u=2, e=2))
             )
+            q_raw.append(load("q_raw%d" % c, q[c].rearrange("(p a) k -> p a k", a=TILES)))
         b1_sb = const.tile([P, PARTS, 16], BF16, name="b1_sb")
         for c in range(PARTS):
             nc.sync.dma_start(
@@ -162,8 +162,10 @@ def tile_qmlp_kernel(
             )
             h_mx[o] = quantise(grouped, "h%d" % o)
 
-        def prepare_w2(w):
-            grouped = transpose_component(w2_raw[w], "w2_grouped%d" % w)
+        def transpose_w2(w):
+            return transpose_component(w2_raw[w], "w2_grouped%d" % w)
+
+        def quantise_w2(w, grouped):
             if w > 0:
                 w2_mx[(w, -1)] = quantise(negate(grouped, "w2_minus%d" % w), "w2_minus%d" % w)
             w2_mx[(w, 1)] = quantise(grouped, "w2_plus%d" % w)
@@ -177,13 +179,21 @@ def tile_qmlp_kernel(
                 out=outs[o].rearrange("(p a) n -> p a n", a=TILES)[:, a, :], in_=result[:]
             )
 
-        q_grouped = {0: transpose_component(q_raw[0], "q_grouped0")}
-        w1_grouped = {0: transpose_component(w1_raw[0], "w1_grouped0")}
+        def transpose_pair(c):
+            w1_grouped[c] = transpose_component(w1_raw[c], "w1_grouped%d" % c)
+            q_grouped[c] = transpose_component(q_raw[c], "q_grouped%d" % c)
+
+        q_grouped = {}
+        w1_grouped = {}
+        w2_grouped = {}
+        transpose_pair(0)
         acc_r = [psum.tile([P, SIZE], F32, name="acc_r%d" % t, tag="bank") for t in range(TILES)]
         for c in range(PARTS):
             if c + 1 < PARTS:
-                q_grouped[c + 1] = transpose_component(q_raw[c + 1], "q_grouped%d" % (c + 1))
-                w1_grouped[c + 1] = transpose_component(w1_raw[c + 1], "w1_grouped%d" % (c + 1))
+                transpose_pair(c + 1)
+            else:
+                w2_grouped[0] = transpose_w2(0)
+                w2_grouped[1] = transpose_w2(1)
             if c > 0:
                 minus = negate(w1_grouped[c], "w1_minus%d" % c)
             q_mx[c] = quantise(q_grouped[c], "q%d" % c)
@@ -192,6 +202,8 @@ def tile_qmlp_kernel(
             w1_mx[(c, 1)] = quantise(w1_grouped[c], "w1_plus%d" % c)
             for t in range(TILES):
                 layer1_pass(acc_r[t], 0, t, c)
+        quantise_w2(0, w2_grouped[0])
+        quantise_w2(1, w2_grouped[1])
         planar = planar_pool.tile([P, TILES, SIZE], BF16, name="planar", tag="planar")
         for t in range(TILES):
             hidden_out_of_psum(acc_r[t], planar, 0, t)
@@ -206,11 +218,11 @@ def tile_qmlp_kernel(
                 hidden_out_of_psum(acc, planar, o, t)
             quantise_hidden(planar, o)
 
-        prepare_w2(0)
-        prepare_w2(1)
         layer1_component(1)
-        prepare_w2(2)
-        prepare_w2(3)
+        w2_grouped[2] = transpose_w2(2)
+        w2_grouped[3] = transpose_w2(3)
+        quantise_w2(2, w2_grouped[2])
+        quantise_w2(3, w2_grouped[3])
         layer1_component(2)
         layer1_component(3)
 

from contextlib import ExitStack

import concourse.mybir as mybir
from concourse.masks import make_identity

F32 = mybir.dt.float32
BF16 = mybir.dt.bfloat16
U32 = mybir.dt.uint32
U8 = mybir.dt.uint8
FP8X4 = mybir.dt.float8_e4m3fn_x4

P = 128
SIZE = 512
TILES = SIZE // P
PACK = 4
PARTS = 4

FLOPS = 2 * 2 * SIZE * (PARTS * SIZE) * (PARTS * SIZE)

HAMILTON = (
    ((0, 1), (1, -1), (2, -1), (3, -1)),
    ((1, 1), (0, 1), (3, 1), (2, -1)),
    ((2, 1), (3, -1), (0, 1), (1, 1)),
    ((3, 1), (2, 1), (1, -1), (0, 1)),
)


def tile_qmlp_kernel(
    tc,
    q_r, q_i, q_j, q_k,
    W1_r, W1_i, W1_j, W1_k,
    b1_r, b1_i, b1_j, b1_k,
    W2_r, W2_i, W2_j, W2_k,
    b2_r, b2_i, b2_j, b2_k,
    out_0, out_1, out_2, out_3,
):
    nc = tc.nc
    q = (q_r, q_i, q_j, q_k)
    w1 = (W1_r, W1_i, W1_j, W1_k)
    b1 = (b1_r, b1_i, b1_j, b1_k)
    w2 = (W2_r, W2_i, W2_j, W2_k)
    b2 = (b2_r, b2_i, b2_j, b2_k)
    outs = (out_0, out_1, out_2, out_3)

    with ExitStack() as ctx:
        const = ctx.enter_context(tc.tile_pool(name="const", bufs=1))
        raw_pool = ctx.enter_context(tc.tile_pool(name="raw", bufs=1))
        grouped_pool = ctx.enter_context(tc.tile_pool(name="grouped", bufs=8))
        planar_pool = ctx.enter_context(tc.tile_pool(name="planar", bufs=2))
        mx_pool = ctx.enter_context(tc.tile_pool(name="mx", bufs=1))
        result_pool = ctx.enter_context(tc.tile_pool(name="result", bufs=4))
        psum = ctx.enter_context(tc.psum_pool(name="psum", bufs=8))
        ctx.enter_context(tc.manual_schedule())

        def load(name, view):
            raw = raw_pool.tile([P, TILES * SIZE], BF16, name=name)
            nc.sync.dma_start(out=raw[:].rearrange("p (n x) -> p n x", n=view.shape[1]), in_=view)
            return raw

        q_raw = []
        w1_raw = []
        for c in range(PARTS):
            w1_raw.append(
                load("w1_raw%d" % c, w1[c].rearrange("(u p e) k -> p u (e k)", u=2, e=2))
            )
            q_raw.append(load("q_raw%d" % c, q[c].rearrange("(p a) k -> p a k", a=TILES)))
        b1_sb = const.tile([P, PARTS, 16], BF16, name="b1_sb")
        for c in range(PARTS):
            nc.sync.dma_start(
                out=b1_sb[:, c, 0:TILES].rearrange("p (u e) -> p u e", u=2),
                in_=b1[c].rearrange("(u p e) -> p u e", u=2, e=2),
            )
        w2_raw = [
            load("w2_raw%d" % c, w2[c].rearrange("(a p) k -> p a k", p=P)) for c in range(PARTS)
        ]
        b2_sb = const.tile([P, PARTS, SIZE], BF16, name="b2_sb")
        for c in range(PARTS):
            nc.sync.dma_start(out=b2_sb[:, c, :], in_=b2[c].partition_broadcast(P))

        ident = const.tile([P, P], F32, name="ident")
        make_identity(nc, ident[:])

        def transpose_component(raw, name):
            words = raw[:].bitcast(F32)
            grouped = grouped_pool.tile(
                [P, SIZE * PACK], BF16, name=name, tag="grouped", align_bytes=64
            )
            grouped_words = grouped[:].bitcast(F32)
            half = SIZE
            for b in range(2):
                bank = psum.tile([P, SIZE], F32, name="%s_bank%d" % (name, b), tag="bank")
                for u in range(2):
                    for a2 in range(2):
                        start = (2 * b + a2) * 2 * P + u * P
                        nc.tensor.transpose(
                            bank[:, (2 * u + a2) * P : (2 * u + a2 + 1) * P],
                            words[:, start : start + P],
                            ident[:],
                        )
                nc.scalar.copy(
                    out=grouped_words[:, b * half : (b + 1) * half].rearrange(
                        "p (n u) -> p n u", u=2
                    ),
                    in_=bank[:].rearrange("p (u n) -> p n u", u=2),
                )
            return grouped

        def negate(grouped, name):
            minus = grouped_pool.tile(
                [P, SIZE * PACK], BF16, name=name, tag="grouped", align_bytes=64
            )
            nc.vector.tensor_scalar_mul(out=minus[:], in0=grouped[:], scalar1=-1.0)
            return minus

        def quantise(grouped, name):
            codes = mx_pool.tile([P, SIZE], U32, name=name + "_codes", align_bytes=64)
            scales = mx_pool.tile([P, SIZE], U8, name=name + "_scales", align_bytes=64)
            nc.vector.quantize_mx(out=codes[:].bitcast(FP8X4), scales=scales[:], in_=grouped[:])
            return codes, scales

        def mx_pass(acc, stationary, tile_index, moving, c):
            s_codes, s_scales = stationary
            m_codes, m_scales = moving
            cols = slice(tile_index * P, (tile_index + 1) * P)
            nc.tensor.matmul_mx(
                out=acc[:],
                lhsT=s_codes[:, cols].bitcast(FP8X4),
                lhsT_scale=s_scales[:, cols],
                rhs=m_codes[:].bitcast(FP8X4),
                rhs_scale=m_scales[:],
                start=(c == 0),
                stop=(c == PARTS - 1),
            )

        q_mx = {}
        w1_mx = {}
        w2_mx = {}
        h_mx = {}

        def layer1_pass(acc, o, t, c):
            mx_pass(acc, w1_mx[HAMILTON[o][c]], t, q_mx[c], c)

        def layer2_pass(acc, a, o, c):
            mx_pass(acc, h_mx[c], a, w2_mx[HAMILTON[o][c]], c)

        def hidden_out_of_psum(acc, planar, o, t):
            nc.scalar.activation(
                out=planar[:, t, :],
                in_=acc[:],
                func=mybir.ActivationFunctionType.Relu,
                bias=b1_sb[:, o, t : t + 1],
                scale=1.0,
            )

        def quantise_hidden(planar, o):
            grouped = grouped_pool.tile(
                [P, SIZE * PACK], BF16, name="h_grouped%d" % o, tag="grouped", align_bytes=64
            )
            nc.vector.tensor_copy(
                out=grouped[:].rearrange("p (n i t) -> p n t i", i=4, t=PACK),
                in_=planar[:].rearrange("p t (n i) -> p n t i", i=4),
            )
            h_mx[o] = quantise(grouped, "h%d" % o)

        def transpose_w2(w):
            return transpose_component(w2_raw[w], "w2_grouped%d" % w)

        def quantise_w2(w, grouped):
            if w > 0:
                w2_mx[(w, -1)] = quantise(negate(grouped, "w2_minus%d" % w), "w2_minus%d" % w)
            w2_mx[(w, 1)] = quantise(grouped, "w2_plus%d" % w)

        def store_output(acc, a, o):
            result = result_pool.tile([P, SIZE], F32, name="result", tag="result")
            nc.vector.tensor_tensor(
                out=result[:], in0=acc[:], in1=b2_sb[:, o, :], op=mybir.AluOpType.add
            )
            nc.sync.dma_start(
                out=outs[o].rearrange("(p a) n -> p a n", a=TILES)[:, a, :], in_=result[:]
            )

        def transpose_pair(c):
            w1_grouped[c] = transpose_component(w1_raw[c], "w1_grouped%d" % c)
            q_grouped[c] = transpose_component(q_raw[c], "q_grouped%d" % c)

        q_grouped = {}
        w1_grouped = {}
        w2_grouped = {}
        transpose_pair(0)
        acc_r = [psum.tile([P, SIZE], F32, name="acc_r%d" % t, tag="bank") for t in range(TILES)]
        for c in range(PARTS):
            if c + 1 < PARTS:
                transpose_pair(c + 1)
            else:
                w2_grouped[0] = transpose_w2(0)
                w2_grouped[1] = transpose_w2(1)
            if c > 0:
                minus = negate(w1_grouped[c], "w1_minus%d" % c)
            q_mx[c] = quantise(q_grouped[c], "q%d" % c)
            if c > 0:
                w1_mx[(c, -1)] = quantise(minus, "w1_minus%d" % c)
            w1_mx[(c, 1)] = quantise(w1_grouped[c], "w1_plus%d" % c)
            for t in range(TILES):
                layer1_pass(acc_r[t], 0, t, c)
        quantise_w2(0, w2_grouped[0])
        quantise_w2(1, w2_grouped[1])
        planar = planar_pool.tile([P, TILES, SIZE], BF16, name="planar", tag="planar")
        for t in range(TILES):
            hidden_out_of_psum(acc_r[t], planar, 0, t)
        quantise_hidden(planar, 0)

        def layer1_component(o):
            planar = planar_pool.tile([P, TILES, SIZE], BF16, name="planar", tag="planar")
            for t in range(TILES):
                acc = psum.tile([P, SIZE], F32, name="acc1", tag="bank")
                for c in range(PARTS):
                    layer1_pass(acc, o, t, c)
                hidden_out_of_psum(acc, planar, o, t)
            quantise_hidden(planar, o)

        layer1_component(1)
        w2_grouped[2] = transpose_w2(2)
        w2_grouped[3] = transpose_w2(3)
        quantise_w2(2, w2_grouped[2])
        quantise_w2(3, w2_grouped[3])
        layer1_component(2)
        layer1_component(3)

        acc_0 = [psum.tile([P, SIZE], F32, name="acc_0%d" % o, tag="bank") for o in range(PARTS)]
        for c in range(PARTS):
            for o in range(PARTS):
                layer2_pass(acc_0[o], 0, o, c)
        for o in range(PARTS):
            store_output(acc_0[o], 0, o)
        for a in range(1, TILES):
            for o in range(PARTS):
                acc = psum.tile([P, SIZE], F32, name="acc2", tag="bank")
                for c in range(PARTS):
                    layer2_pass(acc, a, o, c)
                store_output(acc, a, o)
